import numpy as np
import ml_dtypes

BF16 = ml_dtypes.bfloat16


def bf(x):
    return np.asarray(x, np.float32).astype(BF16)


def f32(x):
    return np.asarray(x, np.float32)


def f64(x):
    return np.asarray(x).astype(np.float64)


def striped(idx):
    return np.tile(idx.reshape(-1, 16).T, (8, 1))


K, M, Q, S, E, A, N = 128, 128, 128, 4096, 512, 6, 3072
ALPHA = 0.2


def elu(v):
    return np.maximum(v, 0.0) + np.exp(np.minimum(v, 0.0)) - 1.0


def setup_inputs():
    return {"table": bf(np.random.standard_normal((K, S))), "w": bf(np.random.standard_normal((K, M)) / np.sqrt(K)), "att": bf(np.random.standard_normal((M, 1)) / np.sqrt(M)), "w2": bf(2.0 * np.random.standard_normal((M, Q)) / np.sqrt(M)), "offs": striped(np.random.permutation(np.tile(np.arange(S), 2))[:N])}


def reference(table, w, att, w2, offs):
    idx = offs[:16].T.reshape(-1)
    y = f64(w).T @ f64(table)[:, idx]
    sc = (f64(att) * y).sum(axis=0)
    lk = np.maximum(sc, ALPHA * sc)
    ex = np.exp(lk).reshape(A, E)
    p = ex / ex.sum(axis=0, keepdims=True)
    pool = (y.reshape(M, A, E) * p[None, :, :]).sum(axis=1)
    h = elu(pool)
    return elu(f64(w2).T @ h)

@@ -1,0 +1,140 @@
+import concourse.mybir as mybir
+from concourse.masks import make_identity
+
+BF16, F32, U16 = mybir.dt.bfloat16, mybir.dt.float32, mybir.dt.uint16
+ACT = mybir.ActivationFunctionType
+ALU = mybir.AluOpType
+AXIS = mybir.AxisListType
+
+P = 128
+NODES = 4096
+EDGES = 512
+MEMBERS = 6
+BLOCK = 128
+N_BLOCKS = EDGES // BLOCK
+PER_BANK = 4
+N_BANKS = N_BLOCKS * MEMBERS // PER_BANK
+PSUM_BANKS = 8
+SLOPE = 0.2
+
+FLOPS = 2 * P * P * MEMBERS * EDGES + 2 * P * MEMBERS * EDGES + 2 * P * P * EDGES
+
+
+def elu(nc, pool, result, value, name):
+    negative = pool.tile([P, EDGES], F32, name=name + "_negative")
+    nc.vector.tensor_scalar_min(negative[:], value, 0.0)
+    grown = pool.tile([P, EDGES], F32, name=name + "_grown")
+    nc.scalar.activation(grown[:], negative[:], ACT.Exp)
+    nc.vector.scalar_tensor_tensor(result, grown[:], -1.0, value, op0=ALU.add, op1=ALU.max)
+
+
+def tile_hypergat_kernel(tc, table, w, att, w2, offs, out):
+    nc = tc.nc
+    with (
+        tc.tile_pool(name="held", bufs=1) as held,
+        tc.psum_pool(name="psum", bufs=1) as psum,
+    ):
+        offsets = held.tile([P, MEMBERS * EDGES // 16], U16, name="offsets")
+        nc.sync.dma_start(offsets[:], offs)
+        table_sb = held.tile([P, NODES], BF16, name="table_sb")
+        nc.sync.dma_start(table_sb[:], table)
+        w_sb = held.tile([P, P], BF16, name="w_sb")
+        nc.scalar.dma_start(w_sb[:], w)
+        att_sb = held.tile([P, 1], BF16, name="att_sb")
+        nc.scalar.dma_start(att_sb[:], att)
+        w2_sb = held.tile([P, P], BF16, name="w2_sb")
+        nc.scalar.dma_start(w2_sb[:], w2)
+        identity = held.tile([P, P], F32, name="identity")
+        make_identity(nc, identity[:])
+
+        y_f32 = []
+        y_bf16 = []
+        for a in range(MEMBERS):
+            picked = table_sb[:].indirect(offsets[:, a * EDGES // 16 : (a + 1) * EDGES // 16])
+            y_ps = psum.tile([P, EDGES], F32, name="y_ps", tag="bank", bufs=PSUM_BANKS - 1)
+            nc.tensor.matmul(y_ps[:], w_sb[:], picked, start=True, stop=True)
+            y_f32.append(held.tile([P, EDGES], F32, name=f"y_f32_{a}"))
+            nc.scalar.copy(y_f32[a][:], y_ps[:])
+            y_bf16.append(held.tile([P, EDGES], BF16, name=f"y_bf16_{a}"))
+            nc.vector.tensor_copy(y_bf16[a][:], y_f32[a][:])
+
+        scores = psum.tile([P, N_BLOCKS * MEMBERS], F32, name="scores")
+        for a in range(MEMBERS):
+            for b in range(N_BLOCKS):
+                col = b * MEMBERS + a
+                nc.tensor.matmul(
+                    scores[:, col : col + 1],
+                    y_bf16[a][:, b * BLOCK : (b + 1) * BLOCK],
+                    att_sb[:],
+                    start=True,
+                    stop=True,
+                )
+
+        flipped = []
+        for bank in range(N_BANKS):
+            flipped.append(psum.tile([P, PER_BANK * P], F32, name=f"flipped_{bank}", tag="bank", bufs=PSUM_BANKS - 1))
+            for j in range(PER_BANK):
+                b, a = divmod(bank * PER_BANK + j, MEMBERS)
+                nc.tensor.transpose(
+                    flipped[bank][:, j * P : (j + 1) * P], y_f32[a][:, b * BLOCK : (b + 1) * BLOCK], identity[:]
+                )
+
+        def by_block(tile):
+            return tile[:].rearrange("p (b a) -> p b a", a=MEMBERS)
+
+        def to_members(tile):
+            return tile[:].unsqueeze(2).to_broadcast([P, N_BLOCKS, MEMBERS])
+
+        damped = held.tile([P, N_BLOCKS * MEMBERS], F32, name="damped")
+        nc.vector.tensor_scalar_mul(damped[:], scores[:], SLOPE)
+        leaky = held.tile([P, N_BLOCKS * MEMBERS], F32, name="leaky")
+        nc.vector.tensor_max(leaky[:], scores[:], damped[:])
+        top = held.tile([P, N_BLOCKS], F32, name="top")
+        nc.vector.reduce_max(top[:], by_block(leaky), axis=AXIS.X)
+        shifted = held.tile([P, N_BLOCKS * MEMBERS], F32, name="shifted")
+        nc.vector.tensor_sub(by_block(shifted), by_block(leaky), to_members(top))
+        grown = held.tile([P, N_BLOCKS * MEMBERS], F32, name="grown")
+        nc.scalar.activation(grown[:], shifted[:], ACT.Exp)
+        total = held.tile([P, N_BLOCKS], F32, name="total")
+        nc.vector.reduce_sum(total[:], by_block(grown), axis=AXIS.X)
+        inverse = held.tile([P, N_BLOCKS], F32, name="inverse")
+        nc.vector.reciprocal(inverse[:], total[:])
+        weight = held.tile([P, N_BLOCKS * MEMBERS], F32, name="weight")
+        nc.vector.tensor_mul(by_block(weight), by_block(grown), to_members(inverse))
+
+        pool_ps = psum.tile([P, EDGES], F32, name="pool_ps", tag="bank", bufs=PSUM_BANKS - 1)
+        for bank in range(N_BANKS):
+            first = bank * PER_BANK
+            weighted = held.tile([P, PER_BANK * P], F32, name=f"weighted_{bank}")
+            if bank % 2 == 0:
+                nc.vector.tensor_mul(
+                    weighted[:].rearrange("p (j m) -> p j m", j=PER_BANK),
+                    flipped[bank][:].rearrange("p (j m) -> p j m", j=PER_BANK),
+                    weight[:, first : first + PER_BANK].unsqueeze(2).to_broadcast([P, PER_BANK, P]),
+                )
+            else:
+                for j in range(PER_BANK):
+                    nc.scalar.activation(
+                        weighted[:, j * P : (j + 1) * P],
+                        flipped[bank][:, j * P : (j + 1) * P],
+                        ACT.Copy,
+                        scale=weight[:, first + j : first + j + 1],
+                    )
+            for j in range(PER_BANK):
+                b, a = divmod(first + j, MEMBERS)
+                nc.tensor.matmul(
+                    pool_ps[:, b * BLOCK : (b + 1) * BLOCK],
+                    weighted[:, j * P : (j + 1) * P],
+                    identity[:],
+                    is_transpose=True,
+                    start=(a == 0),
+                    stop=(a == MEMBERS - 1),
+                )
+
+        h = held.tile([P, EDGES], BF16, name="h")
+        elu(nc, held, h[:], pool_ps[:], "h")
+        out_ps = psum.tile([P, EDGES], F32, name="out_ps", tag="bank", bufs=PSUM_BANKS - 1)
+        nc.tensor.matmul(out_ps[:], w2_sb[:], h[:], start=True, stop=True)
+        out_sb = held.tile([P, EDGES], F32, name="out_sb")
+        elu(nc, held, out_sb[:], out_ps[:], "out")
+        nc.sync.dma_start(out, out_sb[:])

@@ -14,18 +14,25 @@ BLOCK = 128
 N_BLOCKS = EDGES // BLOCK
 PER_BANK = 4
 N_BANKS = N_BLOCKS * MEMBERS // PER_BANK
-PSUM_BANKS = 8
+HALVES = 2
+HALF = EDGES // HALVES
+WIDE_BANKS = 7
+TABLE_LOADS = 4
+WARM_UP = 10
 SLOPE = 0.2
 
 FLOPS = 2 * P * P * MEMBERS * EDGES + 2 * P * MEMBERS * EDGES + 2 * P * P * EDGES
 
 
-def elu(nc, pool, result, value, name):
-    negative = pool.tile([P, EDGES], F32, name=name + "_negative")
-    nc.vector.tensor_scalar_min(negative[:], value, 0.0)
-    grown = pool.tile([P, EDGES], F32, name=name + "_grown")
-    nc.scalar.activation(grown[:], negative[:], ACT.Exp)
-    nc.vector.scalar_tensor_tensor(result, grown[:], -1.0, value, op0=ALU.add, op1=ALU.max)
+def elu(nc, pool, results, values, name):
+    grown, kept = [], []
+    for i, value in enumerate(values):
+        grown.append(pool.tile([P, HALF], F32, name=f"{name}_grown_{i}"))
+        nc.scalar.activation(grown[i][:], value, ACT.Exp)
+        kept.append(pool.tile([P, HALF], F32, name=f"{name}_kept_{i}"))
+        nc.scalar.activation(kept[i][:], value, ACT.Relu)
+    for i, result in enumerate(results):
+        nc.vector.scalar_tensor_tensor(result, grown[i][:], -1.0, kept[i][:], op0=ALU.add, op1=ALU.min)
 
 
 def tile_hypergat_kernel(tc, table, w, att, w2, offs, out):
@@ -34,29 +41,44 @@ def tile_hypergat_kernel(tc, table, w, att, w2, offs, out):
         tc.tile_pool(name="held", bufs=1) as held,
         tc.psum_pool(name="psum", bufs=1) as psum,
     ):
+
+        def wide_bank(name):
+            return psum.tile([P, EDGES], F32, name=name, tag="wide", bufs=WIDE_BANKS)
+
         offsets = held.tile([P, MEMBERS * EDGES // 16], U16, name="offsets")
         nc.sync.dma_start(offsets[:], offs)
-        table_sb = held.tile([P, NODES], BF16, name="table_sb")
-        nc.sync.dma_start(table_sb[:], table)
         w_sb = held.tile([P, P], BF16, name="w_sb")
         nc.scalar.dma_start(w_sb[:], w)
+        table_sb = held.tile([P, NODES], BF16, name="table_sb")
+        part = NODES // TABLE_LOADS
+        for i in range(TABLE_LOADS):
+            queue = nc.sync if i % 2 == 0 else nc.scalar
+            queue.dma_start(table_sb[:, i * part : (i + 1) * part], table[:, i * part : (i + 1) * part])
         att_sb = held.tile([P, 1], BF16, name="att_sb")
-        nc.scalar.dma_start(att_sb[:], att)
+        nc.sync.dma_start(att_sb[:], att)
         w2_sb = held.tile([P, P], BF16, name="w2_sb")
         nc.scalar.dma_start(w2_sb[:], w2)
         identity = held.tile([P, P], F32, name="identity")
         make_identity(nc, identity[:])
 
+        zeros = held.tile([P, EDGES], BF16, name="zeros")
+        nc.vector.memset(zeros[:], 0.0)
+        warm_ps = wide_bank("warm_ps")
+        for i in range(WARM_UP):
+            nc.tensor.matmul(warm_ps[:], zeros[:, 0:P], zeros[:], start=True, stop=True)
+        one = held.tile([P, 1], F32, name="one")
+        nc.scalar.activation(one[:], zeros[:, 0:1], ACT.Exp)
+
         y_f32 = []
         y_bf16 = []
         for a in range(MEMBERS):
             picked = table_sb[:].indirect(offsets[:, a * EDGES // 16 : (a + 1) * EDGES // 16])
-            y_ps = psum.tile([P, EDGES], F32, name="y_ps", tag="bank", bufs=PSUM_BANKS - 1)
+            y_ps = wide_bank("y_ps")
             nc.tensor.matmul(y_ps[:], w_sb[:], picked, start=True, stop=True)
+            y_bf16.append(held.tile([P, EDGES], BF16, name=f"y_bf16_{a}"))
+            nc.vector.tensor_copy(y_bf16[a][:], y_ps[:])
             y_f32.append(held.tile([P, EDGES], F32, name=f"y_f32_{a}"))
             nc.scalar.copy(y_f32[a][:], y_ps[:])
-            y_bf16.append(held.tile([P, EDGES], BF16, name=f"y_bf16_{a}"))
-            nc.vector.tensor_copy(y_bf16[a][:], y_f32[a][:])
 
         scores = psum.tile([P, N_BLOCKS * MEMBERS], F32, name="scores")
         for a in range(MEMBERS):
@@ -72,7 +94,7 @@ def tile_hypergat_kernel(tc, table, w, att, w2, offs, out):
 
         flipped = []
         for bank in range(N_BANKS):
-            flipped.append(psum.tile([P, PER_BANK * P], F32, name=f"flipped_{bank}", tag="bank", bufs=PSUM_BANKS - 1))
+            flipped.append(wide_bank(f"flipped_{bank}"))
             for j in range(PER_BANK):
                 b, a = divmod(bank * PER_BANK + j, MEMBERS)
                 nc.tensor.transpose(
@@ -82,31 +104,38 @@ def tile_hypergat_kernel(tc, table, w, att, w2, offs, out):
         def by_block(tile):
             return tile[:].rearrange("p (b a) -> p b a", a=MEMBERS)
 
-        def to_members(tile):
-            return tile[:].unsqueeze(2).to_broadcast([P, N_BLOCKS, MEMBERS])
-
+        neg_top = held.tile([P, N_BLOCKS], F32, name="neg_top")
+        nc.vector.reduce_max(neg_top[:], by_block(scores), axis=AXIS.X, negate=True)
         damped = held.tile([P, N_BLOCKS * MEMBERS], F32, name="damped")
         nc.vector.tensor_scalar_mul(damped[:], scores[:], SLOPE)
+        neg_peak = held.tile([P, N_BLOCKS], F32, name="neg_peak")
+        nc.vector.scalar_tensor_tensor(neg_peak[:], neg_top[:], SLOPE, neg_top[:], op0=ALU.mult, op1=ALU.min)
         leaky = held.tile([P, N_BLOCKS * MEMBERS], F32, name="leaky")
         nc.vector.tensor_max(leaky[:], scores[:], damped[:])
-        top = held.tile([P, N_BLOCKS], F32, name="top")
-        nc.vector.reduce_max(top[:], by_block(leaky), axis=AXIS.X)
-        shifted = held.tile([P, N_BLOCKS * MEMBERS], F32, name="shifted")
-        nc.vector.tensor_sub(by_block(shifted), by_block(leaky), to_members(top))
         grown = held.tile([P, N_BLOCKS * MEMBERS], F32, name="grown")
-        nc.scalar.activation(grown[:], shifted[:], ACT.Exp)
         total = held.tile([P, N_BLOCKS], F32, name="total")
-        nc.vector.reduce_sum(total[:], by_block(grown), axis=AXIS.X)
+        for b in range(N_BLOCKS):
+            nc.scalar.activation(
+                grown[:, b * MEMBERS : (b + 1) * MEMBERS],
+                leaky[:, b * MEMBERS : (b + 1) * MEMBERS],
+                ACT.Exp,
+                bias=neg_peak[:, b : b + 1],
+                accum_out=total[:, b : b + 1],
+            )
         inverse = held.tile([P, N_BLOCKS], F32, name="inverse")
         nc.vector.reciprocal(inverse[:], total[:])
         weight = held.tile([P, N_BLOCKS * MEMBERS], F32, name="weight")
-        nc.vector.tensor_mul(by_block(weight), by_block(grown), to_members(inverse))
+        nc.vector.tensor_mul(
+            by_block(weight), by_block(grown), inverse[:].unsqueeze(2).to_broadcast([P, N_BLOCKS, MEMBERS])
+        )
 
-        pool_ps = psum.tile([P, EDGES], F32, name="pool_ps", tag="bank", bufs=PSUM_BANKS - 1)
+        pool_ps = []
         for bank in range(N_BANKS):
+            if bank % (N_BANKS // HALVES) == 0:
+                pool_ps.append(wide_bank(f"pool_ps_{len(pool_ps)}"))
             first = bank * PER_BANK
             weighted = held.tile([P, PER_BANK * P], F32, name=f"weighted_{bank}")
-            if bank % 2 == 0:
+            if bank % 3 != 1:
                 nc.vector.tensor_mul(
                     weighted[:].rearrange("p (j m) -> p j m", j=PER_BANK),
                     flipped[bank][:].rearrange("p (j m) -> p j m", j=PER_BANK),
@@ -122,8 +151,9 @@ def tile_hypergat_kernel(tc, table, w, att, w2, offs, out):
                     )
             for j in range(PER_BANK):
                 b, a = divmod(first + j, MEMBERS)
+                half, at = divmod(b * BLOCK, HALF)
                 nc.tensor.matmul(
-                    pool_ps[:, b * BLOCK : (b + 1) * BLOCK],
+                    pool_ps[half][:, at : at + BLOCK],
                     weighted[:, j * P : (j + 1) * P],
                     identity[:],
                     is_transpose=True,
@@ -131,10 +161,13 @@ def tile_hypergat_kernel(tc, table, w, att, w2, offs, out):
                     stop=(a == MEMBERS - 1),
                 )
 
-        h = held.tile([P, EDGES], BF16, name="h")
-        elu(nc, held, h[:], pool_ps[:], "h")
-        out_ps = psum.tile([P, EDGES], F32, name="out_ps", tag="bank", bufs=PSUM_BANKS - 1)
-        nc.tensor.matmul(out_ps[:], w2_sb[:], h[:], start=True, stop=True)
-        out_sb = held.tile([P, EDGES], F32, name="out_sb")
-        elu(nc, held, out_sb[:], out_ps[:], "out")
-        nc.sync.dma_start(out, out_sb[:])
+        h = [held.tile([P, HALF], BF16, name=f"h_{half}") for half in range(HALVES)]
+        elu(nc, held, [t[:] for t in h], [t[:, 0:HALF] for t in pool_ps], "h")
+        out_ps = [wide_bank(f"out_ps_{half}") for half in range(HALVES)]
+        for half in range(HALVES):
+            nc.tensor.matmul(out_ps[half][:, 0:HALF], w2_sb[:], h[half][:], start=True, stop=True)
+        out_sb = [held.tile([P, HALF], F32, name=f"out_sb_{half}") for half in range(HALVES)]
+        elu(nc, held, [t[:] for t in out_sb], [t[:, 0:HALF] for t in out_ps], "out")
+        for half in range(HALVES):
+            queue = nc.sync if half % 2 == 0 else nc.scalar
+            queue.dma_start(out[:, half * HALF : (half + 1) * HALF], out_sb[half][:])

@@ -18,7 +18,7 @@ HALVES = 2
 HALF = EDGES // HALVES
 WIDE_BANKS = 7
 TABLE_LOADS = 4
-WARM_UP = 10
+WARM_UP = 6
 SLOPE = 0.2
 
 FLOPS = 2 * P * P * MEMBERS * EDGES + 2 * P * MEMBERS * EDGES + 2 * P * P * EDGES

@@ -14,8 +14,8 @@ BLOCK = 128
 N_BLOCKS = EDGES // BLOCK
 PER_BANK = 4
 N_BANKS = N_BLOCKS * MEMBERS // PER_BANK
-HALVES = 2
-HALF = EDGES // HALVES
+PARTS = 4
+PART = EDGES // PARTS
 WIDE_BANKS = 7
 TABLE_LOADS = 4
 WARM_UP = 6
@@ -27,9 +27,9 @@ FLOPS = 2 * P * P * MEMBERS * EDGES + 2 * P * MEMBERS * EDGES + 2 * P * P * EDGE
 def elu(nc, pool, results, values, name):
     grown, kept = [], []
     for i, value in enumerate(values):
-        grown.append(pool.tile([P, HALF], F32, name=f"{name}_grown_{i}"))
+        grown.append(pool.tile([P, PART], F32, name=f"{name}_grown_{i}"))
         nc.scalar.activation(grown[i][:], value, ACT.Exp)
-        kept.append(pool.tile([P, HALF], F32, name=f"{name}_kept_{i}"))
+        kept.append(pool.tile([P, PART], F32, name=f"{name}_kept_{i}"))
         nc.scalar.activation(kept[i][:], value, ACT.Relu)
     for i, result in enumerate(results):
         nc.vector.scalar_tensor_tensor(result, grown[i][:], -1.0, kept[i][:], op0=ALU.add, op1=ALU.min)
@@ -131,8 +131,6 @@ def tile_hypergat_kernel(tc, table, w, att, w2, offs, out):
 
         pool_ps = []
         for bank in range(N_BANKS):
-            if bank % (N_BANKS // HALVES) == 0:
-                pool_ps.append(wide_bank(f"pool_ps_{len(pool_ps)}"))
             first = bank * PER_BANK
             weighted = held.tile([P, PER_BANK * P], F32, name=f"weighted_{bank}")
             if bank % 3 != 1:
@@ -151,9 +149,11 @@ def tile_hypergat_kernel(tc, table, w, att, w2, offs, out):
                     )
             for j in range(PER_BANK):
                 b, a = divmod(first + j, MEMBERS)
-                half, at = divmod(b * BLOCK, HALF)
+                part, at = divmod(b * BLOCK, PART)
+                if a == 0 and at == 0:
+                    pool_ps.append(wide_bank(f"pool_ps_{part}"))
                 nc.tensor.matmul(
-                    pool_ps[half][:, at : at + BLOCK],
+                    pool_ps[part][:, at : at + BLOCK],
                     weighted[:, j * P : (j + 1) * P],
                     identity[:],
                     is_transpose=True,
@@ -161,13 +161,12 @@ def tile_hypergat_kernel(tc, table, w, att, w2, offs, out):
                     stop=(a == MEMBERS - 1),
                 )
 
-        h = [held.tile([P, HALF], BF16, name=f"h_{half}") for half in range(HALVES)]
-        elu(nc, held, [t[:] for t in h], [t[:, 0:HALF] for t in pool_ps], "h")
-        out_ps = [wide_bank(f"out_ps_{half}") for half in range(HALVES)]
-        for half in range(HALVES):
-            nc.tensor.matmul(out_ps[half][:, 0:HALF], w2_sb[:], h[half][:], start=True, stop=True)
-        out_sb = [held.tile([P, HALF], F32, name=f"out_sb_{half}") for half in range(HALVES)]
-        elu(nc, held, [t[:] for t in out_sb], [t[:, 0:HALF] for t in out_ps], "out")
-        for half in range(HALVES):
-            queue = nc.sync if half % 2 == 0 else nc.scalar
-            queue.dma_start(out[:, half * HALF : (half + 1) * HALF], out_sb[half][:])
+        h = [held.tile([P, PART], BF16, name=f"h_{part}") for part in range(PARTS)]
+        elu(nc, held, [t[:] for t in h], [t[:, 0:PART] for t in pool_ps], "h")
+        out_ps = [wide_bank(f"out_ps_{part}") for part in range(PARTS)]
+        for part in range(PARTS):
+            nc.tensor.matmul(out_ps[part][:, 0:PART], w2_sb[:], h[part][:], start=True, stop=True)
+        out_sb = [held.tile([P, PART], F32, name=f"out_sb_{part}") for part in range(PARTS)]
+        elu(nc, held, [t[:] for t in out_sb], [t[:, 0:PART] for t in out_ps], "out")
+        for part in range(PARTS):
+            nc.sync.dma_start(out[:, part * PART : (part + 1) * PART], out_sb[part][:])

@@ -18,7 +18,7 @@ PARTS = 4
 PART = EDGES // PARTS
 WIDE_BANKS = 7
 TABLE_LOADS = 4
-WARM_UP = 6
+WARM_UP = 14
 SLOPE = 0.2
 
 FLOPS = 2 * P * P * MEMBERS * EDGES + 2 * P * MEMBERS * EDGES + 2 * P * P * EDGES

@@ -18,7 +18,6 @@ PARTS = 4
 PART = EDGES // PARTS
 WIDE_BANKS = 7
 TABLE_LOADS = 4
-WARM_UP = 14
 SLOPE = 0.2
 
 FLOPS = 2 * P * P * MEMBERS * EDGES + 2 * P * MEMBERS * EDGES + 2 * P * P * EDGES
@@ -61,13 +60,10 @@ def tile_hypergat_kernel(tc, table, w, att, w2, offs, out):
         identity = held.tile([P, P], F32, name="identity")
         make_identity(nc, identity[:])
 
-        zeros = held.tile([P, EDGES], BF16, name="zeros")
-        nc.vector.memset(zeros[:], 0.0)
-        warm_ps = wide_bank("warm_ps")
-        for i in range(WARM_UP):
-            nc.tensor.matmul(warm_ps[:], zeros[:, 0:P], zeros[:], start=True, stop=True)
+        zero = held.tile([P, 1], F32, name="zero")
+        nc.vector.memset(zero[:], 0.0)
         one = held.tile([P, 1], F32, name="one")
-        nc.scalar.activation(one[:], zeros[:, 0:1], ACT.Exp)
+        nc.scalar.activation(one[:], zero[:], ACT.Exp)
 
         y_f32 = []
         y_bf16 = []

@@ -18,6 +18,7 @@ PARTS = 4
 PART = EDGES // PARTS
 WIDE_BANKS = 7
 TABLE_LOADS = 4
+REPEAT = 64
 SLOPE = 0.2
 
 FLOPS = 2 * P * P * MEMBERS * EDGES + 2 * P * MEMBERS * EDGES + 2 * P * P * EDGES
@@ -64,6 +65,8 @@ def tile_hypergat_kernel(tc, table, w, att, w2, offs, out):
         nc.vector.memset(zero[:], 0.0)
         one = held.tile([P, 1], F32, name="one")
         nc.scalar.activation(one[:], zero[:], ACT.Exp)
+        att_wide = held.tile([P, REPEAT], BF16, name="att_wide")
+        nc.vector.tensor_copy(att_wide[:], att_sb[:].to_broadcast([P, REPEAT]))
 
         y_f32 = []
         y_bf16 = []
@@ -76,17 +79,18 @@ def tile_hypergat_kernel(tc, table, w, att, w2, offs, out):
             y_f32.append(held.tile([P, EDGES], F32, name=f"y_f32_{a}"))
             nc.scalar.copy(y_f32[a][:], y_ps[:])
 
-        scores = psum.tile([P, N_BLOCKS * MEMBERS], F32, name="scores")
+        scores_ps = psum.tile([P, MEMBERS * N_BLOCKS + REPEAT - 1], F32, name="scores_ps")
         for a in range(MEMBERS):
             for b in range(N_BLOCKS):
-                col = b * MEMBERS + a
+                col = a * N_BLOCKS + b
                 nc.tensor.matmul(
-                    scores[:, col : col + 1],
+                    scores_ps[:, col : col + REPEAT],
                     y_bf16[a][:, b * BLOCK : (b + 1) * BLOCK],
-                    att_sb[:],
+                    att_wide[:],
                     start=True,
                     stop=True,
                 )
+        scores = scores_ps[:, 0 : MEMBERS * N_BLOCKS].rearrange("p (a b) -> p b a", b=N_BLOCKS)
 
         flipped = []
         for bank in range(N_BANKS):
@@ -101,13 +105,13 @@ def tile_hypergat_kernel(tc, table, w, att, w2, offs, out):
             return tile[:].rearrange("p (b a) -> p b a", a=MEMBERS)
 
         neg_top = held.tile([P, N_BLOCKS], F32, name="neg_top")
-        nc.vector.reduce_max(neg_top[:], by_block(scores), axis=AXIS.X, negate=True)
+        nc.vector.reduce_max(neg_top[:], scores, axis=AXIS.X, negate=True)
         damped = held.tile([P, N_BLOCKS * MEMBERS], F32, name="damped")
-        nc.vector.tensor_scalar_mul(damped[:], scores[:], SLOPE)
+        nc.vector.tensor_scalar_mul(by_block(damped), scores, SLOPE)
         neg_peak = held.tile([P, N_BLOCKS], F32, name="neg_peak")
         nc.vector.scalar_tensor_tensor(neg_peak[:], neg_top[:], SLOPE, neg_top[:], op0=ALU.mult, op1=ALU.min)
         leaky = held.tile([P, N_BLOCKS * MEMBERS], F32, name="leaky")
-        nc.vector.tensor_max(leaky[:], scores[:], damped[:])
+        nc.vector.tensor_max(by_block(leaky), scores, by_block(damped))
         grown = held.tile([P, N_BLOCKS * MEMBERS], F32, name="grown")
         total = held.tile([P, N_BLOCKS], F32, name="total")
         for b in range(N_BLOCKS):

@@ -92,13 +92,20 @@ def tile_hypergat_kernel(tc, table, w, att, w2, offs, out):
                 )
         scores = scores_ps[:, 0 : MEMBERS * N_BLOCKS].rearrange("p (a b) -> p b a", b=N_BLOCKS)
 
+        def flip(result, block, counted, start, stop):
+            nc.tensor.matmul(result, block, identity[:], is_transpose=not counted, start=start, stop=stop)
+
         flipped = []
         for bank in range(N_BANKS):
             flipped.append(wide_bank(f"flipped_{bank}"))
             for j in range(PER_BANK):
                 b, a = divmod(bank * PER_BANK + j, MEMBERS)
-                nc.tensor.transpose(
-                    flipped[bank][:, j * P : (j + 1) * P], y_f32[a][:, b * BLOCK : (b + 1) * BLOCK], identity[:]
+                flip(
+                    flipped[bank][:, j * P : (j + 1) * P],
+                    y_f32[a][:, b * BLOCK : (b + 1) * BLOCK],
+                    counted=(j == 0),
+                    start=True,
+                    stop=True,
                 )
 
         def by_block(tile):
@@ -152,11 +159,10 @@ def tile_hypergat_kernel(tc, table, w, att, w2, offs, out):
                 part, at = divmod(b * BLOCK, PART)
                 if a == 0 and at == 0:
                     pool_ps.append(wide_bank(f"pool_ps_{part}"))
-                nc.tensor.matmul(
+                flip(
                     pool_ps[part][:, at : at + BLOCK],
                     weighted[:, j * P : (j + 1) * P],
-                    identity[:],
-                    is_transpose=True,
+                    counted=(a == 0),
                     start=(a == 0),
                     stop=(a == MEMBERS - 1),
                 )

@@ -10,13 +10,17 @@ P = 128
 NODES = 4096
 EDGES = 512
 MEMBERS = 6
+HALVES = 2
+HALF = EDGES // HALVES
 BLOCK = 128
-N_BLOCKS = EDGES // BLOCK
-PER_BANK = 4
-N_BANKS = N_BLOCKS * MEMBERS // PER_BANK
-PARTS = 4
-PART = EDGES // PARTS
-WIDE_BANKS = 7
+BLOCKS = HALF // BLOCK
+BANK = 512
+PSUM_BANKS = 8
+PER_Y = BANK // HALF
+N_Y = MEMBERS // PER_Y
+CHAINS = 3
+LINKS = MEMBERS // CHAINS
+PER_BANK = BANK // P
 TABLE_LOADS = 4
 REPEAT = 64
 SLOPE = 0.2
@@ -27,9 +31,9 @@ FLOPS = 2 * P * P * MEMBERS * EDGES + 2 * P * MEMBERS * EDGES + 2 * P * P * EDGE
 def elu(nc, pool, results, values, name):
     grown, kept = [], []
     for i, value in enumerate(values):
-        grown.append(pool.tile([P, PART], F32, name=f"{name}_grown_{i}"))
+        grown.append(pool.tile([P, BLOCK], F32, name=f"{name}_grown_{i}"))
         nc.scalar.activation(grown[i][:], value, ACT.Exp)
-        kept.append(pool.tile([P, PART], F32, name=f"{name}_kept_{i}"))
+        kept.append(pool.tile([P, BLOCK], F32, name=f"{name}_kept_{i}"))
         nc.scalar.activation(kept[i][:], value, ACT.Relu)
     for i, result in enumerate(results):
         nc.vector.scalar_tensor_tensor(result, grown[i][:], -1.0, kept[i][:], op0=ALU.add, op1=ALU.min)
@@ -42,8 +46,8 @@ def tile_hypergat_kernel(tc, table, w, att, w2, offs, out):
         tc.psum_pool(name="psum", bufs=1) as psum,
     ):
 
-        def wide_bank(name):
-            return psum.tile([P, EDGES], F32, name=name, tag="wide", bufs=WIDE_BANKS)
+        def bank(name):
+            return psum.tile([P, BANK], F32, name=name, tag="bank", bufs=PSUM_BANKS)
 
         offsets = held.tile([P, MEMBERS * EDGES // 16], U16, name="offsets")
         nc.sync.dma_start(offsets[:], offs)
@@ -68,111 +72,113 @@ def tile_hypergat_kernel(tc, table, w, att, w2, offs, out):
         att_wide = held.tile([P, REPEAT], BF16, name="att_wide")
         nc.vector.tensor_copy(att_wide[:], att_sb[:].to_broadcast([P, REPEAT]))
 
-        y_f32 = []
-        y_bf16 = []
-        for a in range(MEMBERS):
-            picked = table_sb[:].indirect(offsets[:, a * EDGES // 16 : (a + 1) * EDGES // 16])
-            y_ps = wide_bank("y_ps")
-            nc.tensor.matmul(y_ps[:], w_sb[:], picked, start=True, stop=True)
-            y_bf16.append(held.tile([P, EDGES], BF16, name=f"y_bf16_{a}"))
-            nc.vector.tensor_copy(y_bf16[a][:], y_ps[:])
-            y_f32.append(held.tile([P, EDGES], F32, name=f"y_f32_{a}"))
-            nc.scalar.copy(y_f32[a][:], y_ps[:])
+        y_f32 = [[] for h in range(HALVES)]
+        y_bf16 = [[] for h in range(HALVES)]
+        for h in range(HALVES):
+            for k in range(N_Y):
+                y_ps = bank(f"y_ps_{h}_{k}")
+                for i in range(PER_Y):
+                    first = ((k * PER_Y + i) * EDGES + h * HALF) // 16
+                    picked = table_sb[:].indirect(offsets[:, first : first + HALF // 16])
+                    nc.tensor.matmul(y_ps[:, i * HALF : (i + 1) * HALF], w_sb[:], picked, start=True, stop=True)
+                y_bf16[h].append(held.tile([P, BANK], BF16, name=f"y_bf16_{h}_{k}"))
+                nc.vector.tensor_copy(y_bf16[h][k][:], y_ps[:])
+                y_f32[h].append(held.tile([P, BANK], F32, name=f"y_f32_{h}_{k}"))
+                nc.scalar.copy(y_f32[h][k][:], y_ps[:])
 
-        scores_ps = psum.tile([P, MEMBERS * N_BLOCKS + REPEAT - 1], F32, name="scores_ps")
-        for a in range(MEMBERS):
-            for b in range(N_BLOCKS):
-                col = a * N_BLOCKS + b
-                nc.tensor.matmul(
-                    scores_ps[:, col : col + REPEAT],
-                    y_bf16[a][:, b * BLOCK : (b + 1) * BLOCK],
-                    att_wide[:],
-                    start=True,
-                    stop=True,
-                )
-        scores = scores_ps[:, 0 : MEMBERS * N_BLOCKS].rearrange("p (a b) -> p b a", b=N_BLOCKS)
+        def y_block(tiles, a, b):
+            k, i = divmod(a, PER_Y)
+            return tiles[k][:, i * HALF + b * BLOCK : i * HALF + (b + 1) * BLOCK]
 
-        def flip(result, block, counted, start, stop):
-            nc.tensor.matmul(result, block, identity[:], is_transpose=not counted, start=start, stop=stop)
+        scores = []
+        for h in range(HALVES):
+            scores_ps = bank(f"scores_ps_{h}")
+            for a in range(MEMBERS):
+                for b in range(BLOCKS):
+                    col = a * BLOCKS + b
+                    nc.tensor.matmul(
+                        scores_ps[:, col : col + REPEAT], y_block(y_bf16[h], a, b), att_wide[:], start=True, stop=True
+                    )
+            scores.append(scores_ps[:, 0 : MEMBERS * BLOCKS].rearrange("p (a b) -> p b a", b=BLOCKS))
 
-        flipped = []
-        for bank in range(N_BANKS):
-            flipped.append(wide_bank(f"flipped_{bank}"))
-            for j in range(PER_BANK):
-                b, a = divmod(bank * PER_BANK + j, MEMBERS)
-                flip(
-                    flipped[bank][:, j * P : (j + 1) * P],
-                    y_f32[a][:, b * BLOCK : (b + 1) * BLOCK],
-                    counted=(j == 0),
-                    start=True,
-                    stop=True,
-                )
+        def flip(result, block, start, stop):
+            nc.tensor.matmul(result, block, identity[:], is_transpose=True, start=start, stop=stop)
+
+        lead = [bank(f"lead_{n}") for n in range(HALVES * BLOCKS * CHAINS // PER_BANK)]
+        rest = [bank(f"rest_{n}") for n in range(HALVES * BLOCKS * (MEMBERS - CHAINS) // PER_BANK)]
+
+        def flipped(h, b, a):
+            c, i = divmod(a, LINKS)
+            if i == 0:
+                n, slot = divmod((h * BLOCKS + b) * CHAINS + c, PER_BANK)
+                return lead[n][:, slot * P : (slot + 1) * P]
+            n, slot = divmod(((h * BLOCKS + b) * CHAINS + c) * (LINKS - 1) + i - 1, PER_BANK)
+            return rest[n][:, slot * P : (slot + 1) * P]
+
+        for h in range(HALVES):
+            for b in range(BLOCKS):
+                for a in range(MEMBERS):
+                    flip(flipped(h, b, a), y_block(y_f32[h], a, b), start=True, stop=True)
 
         def by_block(tile):
             return tile[:].rearrange("p (b a) -> p b a", a=MEMBERS)
 
-        neg_top = held.tile([P, N_BLOCKS], F32, name="neg_top")
-        nc.vector.reduce_max(neg_top[:], scores, axis=AXIS.X, negate=True)
-        damped = held.tile([P, N_BLOCKS * MEMBERS], F32, name="damped")
-        nc.vector.tensor_scalar_mul(by_block(damped), scores, SLOPE)
-        neg_peak = held.tile([P, N_BLOCKS], F32, name="neg_peak")
-        nc.vector.scalar_tensor_tensor(neg_peak[:], neg_top[:], SLOPE, neg_top[:], op0=ALU.mult, op1=ALU.min)
-        leaky = held.tile([P, N_BLOCKS * MEMBERS], F32, name="leaky")
-        nc.vector.tensor_max(by_block(leaky), scores, by_block(damped))
-        grown = held.tile([P, N_BLOCKS * MEMBERS], F32, name="grown")
-        total = held.tile([P, N_BLOCKS], F32, name="total")
-        for b in range(N_BLOCKS):
-            nc.scalar.activation(
-                grown[:, b * MEMBERS : (b + 1) * MEMBERS],
-                leaky[:, b * MEMBERS : (b + 1) * MEMBERS],
-                ACT.Exp,
-                bias=neg_peak[:, b : b + 1],
-                accum_out=total[:, b : b + 1],
+        weight = []
+        for h in range(HALVES):
+            neg_top = held.tile([P, BLOCKS], F32, name=f"neg_top_{h}")
+            nc.vector.reduce_max(neg_top[:], scores[h], axis=AXIS.X, negate=True)
+            damped = held.tile([P, BLOCKS * MEMBERS], F32, name=f"damped_{h}")
+            nc.vector.tensor_scalar_mul(by_block(damped), scores[h], SLOPE)
+            neg_peak = held.tile([P, BLOCKS], F32, name=f"neg_peak_{h}")
+            nc.vector.scalar_tensor_tensor(neg_peak[:], neg_top[:], SLOPE, neg_top[:], op0=ALU.mult, op1=ALU.min)
+            leaky = held.tile([P, BLOCKS * MEMBERS], F32, name=f"leaky_{h}")
+            nc.vector.tensor_max(by_block(leaky), scores[h], by_block(damped))
+            grown = held.tile([P, BLOCKS * MEMBERS], F32, name=f"grown_{h}")
+            total = held.tile([P, BLOCKS], F32, name=f"total_{h}")
+            for b in range(BLOCKS):
+                nc.scalar.activation(
+                    grown[:, b * MEMBERS : (b + 1) * MEMBERS],
+                    leaky[:, b * MEMBERS : (b + 1) * MEMBERS],
+                    ACT.Exp,
+                    bias=neg_peak[:, b : b + 1],
+                    accum_out=total[:, b : b + 1],
+                )
+            inverse = held.tile([P, BLOCKS], F32, name=f"inverse_{h}")
+            nc.vector.reciprocal(inverse[:], total[:])
+            weight.append(held.tile([P, BLOCKS * MEMBERS], F32, name=f"weight_{h}"))
+            nc.vector.tensor_mul(
+                by_block(weight[h]), by_block(grown), inverse[:].unsqueeze(2).to_broadcast([P, BLOCKS, MEMBERS])
             )
-        inverse = held.tile([P, N_BLOCKS], F32, name="inverse")
-        nc.vector.reciprocal(inverse[:], total[:])
-        weight = held.tile([P, N_BLOCKS * MEMBERS], F32, name="weight")
-        nc.vector.tensor_mul(
-            by_block(weight), by_block(grown), inverse[:].unsqueeze(2).to_broadcast([P, N_BLOCKS, MEMBERS])
-        )
 
-        pool_ps = []
-        for bank in range(N_BANKS):
-            first = bank * PER_BANK
-            weighted = held.tile([P, PER_BANK * P], F32, name=f"weighted_{bank}")
-            if bank % 3 != 1:
-                nc.vector.tensor_mul(
-                    weighted[:].rearrange("p (j m) -> p j m", j=PER_BANK),
-                    flipped[bank][:].rearrange("p (j m) -> p j m", j=PER_BANK),
-                    weight[:, first : first + PER_BANK].unsqueeze(2).to_broadcast([P, PER_BANK, P]),
-                )
-            else:
-                for j in range(PER_BANK):
-                    nc.scalar.activation(
-                        weighted[:, j * P : (j + 1) * P],
-                        flipped[bank][:, j * P : (j + 1) * P],
-                        ACT.Copy,
-                        scale=weight[:, first + j : first + j + 1],
-                    )
-            for j in range(PER_BANK):
-                b, a = divmod(first + j, MEMBERS)
-                part, at = divmod(b * BLOCK, PART)
-                if a == 0 and at == 0:
-                    pool_ps.append(wide_bank(f"pool_ps_{part}"))
-                flip(
-                    pool_ps[part][:, at : at + BLOCK],
-                    weighted[:, j * P : (j + 1) * P],
-                    counted=(a == 0),
-                    start=(a == 0),
-                    stop=(a == MEMBERS - 1),
-                )
+        pool_ps = [[] for h in range(HALVES)]
+        for h in range(HALVES):
+            sums = {}
+            for i in range(LINKS):
+                for b in range(BLOCKS):
+                    for c in range(CHAINS):
+                        a = c * LINKS + i
+                        column = weight[h][:, b * MEMBERS + a : b * MEMBERS + a + 1]
+                        longer = held.tile([P, P], F32, name=f"sum_{h}_{b}_{c}_{i}")
+                        if i == 0:
+                            nc.scalar.activation(longer[:], flipped(h, b, a), ACT.Copy, scale=column)
+                        else:
+                            nc.vector.scalar_tensor_tensor(
+                                longer[:], flipped(h, b, a), column, sums[b, c][:], op0=ALU.mult, op1=ALU.add
+                            )
+                        sums[b, c] = longer
+            for b in range(BLOCKS):
+                pool_ps[h].append(bank(f"pool_ps_{h}_{b}"))
+                for c in range(CHAINS):
+                    flip(pool_ps[h][b][:, 0:BLOCK], sums[b, c][:], start=(c == 0), stop=(c == CHAINS - 1))
 
-        h = [held.tile([P, PART], BF16, name=f"h_{part}") for part in range(PARTS)]
-        elu(nc, held, [t[:] for t in h], [t[:, 0:PART] for t in pool_ps], "h")
-        out_ps = [wide_bank(f"out_ps_{part}") for part in range(PARTS)]
-        for part in range(PARTS):
-            nc.tensor.matmul(out_ps[part][:, 0:PART], w2_sb[:], h[part][:], start=True, stop=True)
-        out_sb = [held.tile([P, PART], F32, name=f"out_sb_{part}") for part in range(PARTS)]
-        elu(nc, held, [t[:] for t in out_sb], [t[:, 0:PART] for t in out_ps], "out")
-        for part in range(PARTS):
-            nc.sync.dma_start(out[:, part * PART : (part + 1) * PART], out_sb[part][:])
+        for h in range(HALVES):
+            hidden = [held.tile([P, BLOCK], BF16, name=f"hidden_{h}_{b}") for b in range(BLOCKS)]
+            elu(nc, held, [t[:] for t in hidden], [t[:, 0:BLOCK] for t in pool_ps[h]], f"hidden_{h}")
+            out_ps = [bank(f"out_ps_{h}_{b}") for b in range(BLOCKS)]
+            for b in range(BLOCKS):
+                nc.tensor.matmul(out_ps[b][:, 0:BLOCK], w2_sb[:], hidden[b][:], start=True, stop=True)
+            out_sb = [held.tile([P, BLOCK], F32, name=f"out_sb_{h}_{b}") for b in range(BLOCKS)]
+            elu(nc, held, [t[:] for t in out_sb], [t[:, 0:BLOCK] for t in out_ps], f"out_{h}")
+            for b in range(BLOCKS):
+                at = h * HALF + b * BLOCK
+                nc.sync.dma_start(out[:, at : at + BLOCK], out_sb[b][:])

@@ -10,7 +10,7 @@ P = 128
 NODES = 4096
 EDGES = 512
 MEMBERS = 6
-HALVES = 2
+HALVES = 1
 HALF = EDGES // HALVES
 BLOCK = 128
 BLOCKS = HALF // BLOCK

@@ -10,17 +10,13 @@ P = 128
 NODES = 4096
 EDGES = 512
 MEMBERS = 6
-HALVES = 1
-HALF = EDGES // HALVES
 BLOCK = 128
-BLOCKS = HALF // BLOCK
+BLOCKS = EDGES // BLOCK
 BANK = 512
 PSUM_BANKS = 8
-PER_Y = BANK // HALF
-N_Y = MEMBERS // PER_Y
+PER_BANK = BANK // P
 CHAINS = 3
 LINKS = MEMBERS // CHAINS
-PER_BANK = BANK // P
 TABLE_LOADS = 4
 REPEAT = 64
 SLOPE = 0.2
@@ -72,113 +68,108 @@ def tile_hypergat_kernel(tc, table, w, att, w2, offs, out):
         att_wide = held.tile([P, REPEAT], BF16, name="att_wide")
         nc.vector.tensor_copy(att_wide[:], att_sb[:].to_broadcast([P, REPEAT]))
 
-        y_f32 = [[] for h in range(HALVES)]
-        y_bf16 = [[] for h in range(HALVES)]
-        for h in range(HALVES):
-            for k in range(N_Y):
-                y_ps = bank(f"y_ps_{h}_{k}")
-                for i in range(PER_Y):
-                    first = ((k * PER_Y + i) * EDGES + h * HALF) // 16
-                    picked = table_sb[:].indirect(offsets[:, first : first + HALF // 16])
-                    nc.tensor.matmul(y_ps[:, i * HALF : (i + 1) * HALF], w_sb[:], picked, start=True, stop=True)
-                y_bf16[h].append(held.tile([P, BANK], BF16, name=f"y_bf16_{h}_{k}"))
-                nc.vector.tensor_copy(y_bf16[h][k][:], y_ps[:])
-                y_f32[h].append(held.tile([P, BANK], F32, name=f"y_f32_{h}_{k}"))
-                nc.scalar.copy(y_f32[h][k][:], y_ps[:])
+        y_f32 = []
+        y_bf16 = []
+        for a in range(MEMBERS):
+            picked = table_sb[:].indirect(offsets[:, a * EDGES // 16 : (a + 1) * EDGES // 16])
+            y_ps = bank(f"y_ps_{a}")
+            nc.tensor.matmul(y_ps[:], w_sb[:], picked, start=True, stop=True)
+            y_bf16.append(held.tile([P, EDGES], BF16, name=f"y_bf16_{a}"))
+            nc.vector.tensor_copy(y_bf16[a][:], y_ps[:])
+            y_f32.append(held.tile([P, EDGES], F32, name=f"y_f32_{a}"))
+            nc.scalar.copy(y_f32[a][:], y_ps[:])
 
-        def y_block(tiles, a, b):
-            k, i = divmod(a, PER_Y)
-            return tiles[k][:, i * HALF + b * BLOCK : i * HALF + (b + 1) * BLOCK]
+        scores_ps = bank("scores_ps")
+        for a in range(MEMBERS):
+            for b in range(BLOCKS):
+                col = a * BLOCKS + b
+                nc.tensor.matmul(
+                    scores_ps[:, col : col + REPEAT],
+                    y_bf16[a][:, b * BLOCK : (b + 1) * BLOCK],
+                    att_wide[:],
+                    start=True,
+                    stop=True,
+                )
+        scores = scores_ps[:, 0 : MEMBERS * BLOCKS].rearrange("p (a b) -> p b a", b=BLOCKS)
 
-        scores = []
-        for h in range(HALVES):
-            scores_ps = bank(f"scores_ps_{h}")
-            for a in range(MEMBERS):
-                for b in range(BLOCKS):
-                    col = a * BLOCKS + b
-                    nc.tensor.matmul(
-                        scores_ps[:, col : col + REPEAT], y_block(y_bf16[h], a, b), att_wide[:], start=True, stop=True
-                    )
-            scores.append(scores_ps[:, 0 : MEMBERS * BLOCKS].rearrange("p (a b) -> p b a", b=BLOCKS))
+        def flip(result, block, start, stop, counted=False):
+            nc.tensor.matmul(result, block, identity[:], is_transpose=not counted, start=start, stop=stop)
 
-        def flip(result, block, start, stop):
-            nc.tensor.matmul(result, block, identity[:], is_transpose=True, start=start, stop=stop)
+        lead = [bank(f"lead_{n}") for n in range(BLOCKS * CHAINS // PER_BANK)]
+        rest = [bank(f"rest_{n}") for n in range(BLOCKS * (MEMBERS - CHAINS) // PER_BANK)]
 
-        lead = [bank(f"lead_{n}") for n in range(HALVES * BLOCKS * CHAINS // PER_BANK)]
-        rest = [bank(f"rest_{n}") for n in range(HALVES * BLOCKS * (MEMBERS - CHAINS) // PER_BANK)]
-
-        def flipped(h, b, a):
+        def flipped(b, a):
             c, i = divmod(a, LINKS)
             if i == 0:
-                n, slot = divmod((h * BLOCKS + b) * CHAINS + c, PER_BANK)
+                n, slot = divmod(b * CHAINS + c, PER_BANK)
                 return lead[n][:, slot * P : (slot + 1) * P]
-            n, slot = divmod(((h * BLOCKS + b) * CHAINS + c) * (LINKS - 1) + i - 1, PER_BANK)
+            n, slot = divmod((b * CHAINS + c) * (LINKS - 1) + i - 1, PER_BANK)
             return rest[n][:, slot * P : (slot + 1) * P]
 
-        for h in range(HALVES):
-            for b in range(BLOCKS):
-                for a in range(MEMBERS):
-                    flip(flipped(h, b, a), y_block(y_f32[h], a, b), start=True, stop=True)
+        for b in range(BLOCKS):
+            for a in range(MEMBERS):
+                flip(
+                    flipped(b, a),
+                    y_f32[a][:, b * BLOCK : (b + 1) * BLOCK],
+                    start=True,
+                    stop=True,
+                    counted=(a == MEMBERS - 1),
+                )
 
         def by_block(tile):
             return tile[:].rearrange("p (b a) -> p b a", a=MEMBERS)
 
-        weight = []
-        for h in range(HALVES):
-            neg_top = held.tile([P, BLOCKS], F32, name=f"neg_top_{h}")
-            nc.vector.reduce_max(neg_top[:], scores[h], axis=AXIS.X, negate=True)
-            damped = held.tile([P, BLOCKS * MEMBERS], F32, name=f"damped_{h}")
-            nc.vector.tensor_scalar_mul(by_block(damped), scores[h], SLOPE)
-            neg_peak = held.tile([P, BLOCKS], F32, name=f"neg_peak_{h}")
-            nc.vector.scalar_tensor_tensor(neg_peak[:], neg_top[:], SLOPE, neg_top[:], op0=ALU.mult, op1=ALU.min)
-            leaky = held.tile([P, BLOCKS * MEMBERS], F32, name=f"leaky_{h}")
-            nc.vector.tensor_max(by_block(leaky), scores[h], by_block(damped))
-            grown = held.tile([P, BLOCKS * MEMBERS], F32, name=f"grown_{h}")
-            total = held.tile([P, BLOCKS], F32, name=f"total_{h}")
-            for b in range(BLOCKS):
-                nc.scalar.activation(
-                    grown[:, b * MEMBERS : (b + 1) * MEMBERS],
-                    leaky[:, b * MEMBERS : (b + 1) * MEMBERS],
-                    ACT.Exp,
-                    bias=neg_peak[:, b : b + 1],
-                    accum_out=total[:, b : b + 1],
-                )
-            inverse = held.tile([P, BLOCKS], F32, name=f"inverse_{h}")
-            nc.vector.reciprocal(inverse[:], total[:])
-            weight.append(held.tile([P, BLOCKS * MEMBERS], F32, name=f"weight_{h}"))
-            nc.vector.tensor_mul(
-                by_block(weight[h]), by_block(grown), inverse[:].unsqueeze(2).to_broadcast([P, BLOCKS, MEMBERS])
+        neg_top = held.tile([P, BLOCKS], F32, name="neg_top")
+        nc.vector.reduce_max(neg_top[:], scores, axis=AXIS.X, negate=True)
+        damped = held.tile([P, BLOCKS * MEMBERS], F32, name="damped")
+        nc.vector.tensor_scalar_mul(by_block(damped), scores, SLOPE)
+        neg_peak = held.tile([P, BLOCKS], F32, name="neg_peak")
+        nc.vector.scalar_tensor_tensor(neg_peak[:], neg_top[:], SLOPE, neg_top[:], op0=ALU.mult, op1=ALU.min)
+        leaky = held.tile([P, BLOCKS * MEMBERS], F32, name="leaky")
+        nc.vector.tensor_max(by_block(leaky), scores, by_block(damped))
+        grown = held.tile([P, BLOCKS * MEMBERS], F32, name="grown")
+        total = held.tile([P, BLOCKS], F32, name="total")
+        for b in range(BLOCKS):
+            nc.scalar.activation(
+                grown[:, b * MEMBERS : (b + 1) * MEMBERS],
+                leaky[:, b * MEMBERS : (b + 1) * MEMBERS],
+                ACT.Exp,
+                bias=neg_peak[:, b : b + 1],
+                accum_out=total[:, b : b + 1],
             )
+        inverse = held.tile([P, BLOCKS], F32, name="inverse")
+        nc.vector.reciprocal(inverse[:], total[:])
+        weight = held.tile([P, BLOCKS * MEMBERS], F32, name="weight")
+        nc.vector.tensor_mul(
+            by_block(weight), by_block(grown), inverse[:].unsqueeze(2).to_broadcast([P, BLOCKS, MEMBERS])
+        )
 
-        pool_ps = [[] for h in range(HALVES)]
-        for h in range(HALVES):
-            sums = {}
-            for i in range(LINKS):
-                for b in range(BLOCKS):
-                    for c in range(CHAINS):
-                        a = c * LINKS + i
-                        column = weight[h][:, b * MEMBERS + a : b * MEMBERS + a + 1]
-                        longer = held.tile([P, P], F32, name=f"sum_{h}_{b}_{c}_{i}")
-                        if i == 0:
-                            nc.scalar.activation(longer[:], flipped(h, b, a), ACT.Copy, scale=column)
-                        else:
-                            nc.vector.scalar_tensor_tensor(
-                                longer[:], flipped(h, b, a), column, sums[b, c][:], op0=ALU.mult, op1=ALU.add
-                            )
-                        sums[b, c] = longer
+        sums = {}
+        for i in range(LINKS):
             for b in range(BLOCKS):
-                pool_ps[h].append(bank(f"pool_ps_{h}_{b}"))
                 for c in range(CHAINS):
-                    flip(pool_ps[h][b][:, 0:BLOCK], sums[b, c][:], start=(c == 0), stop=(c == CHAINS - 1))
+                    a = c * LINKS + i
+                    column = weight[:, b * MEMBERS + a : b * MEMBERS + a + 1]
+                    longer = held.tile([P, P], F32, name=f"sum_{b}_{c}_{i}")
+                    if i == 0:
+                        nc.scalar.activation(longer[:], flipped(b, a), ACT.Copy, scale=column)
+                    else:
+                        nc.vector.scalar_tensor_tensor(
+                            longer[:], flipped(b, a), column, sums[b, c][:], op0=ALU.mult, op1=ALU.add
+                        )
+                    sums[b, c] = longer
+        pool_ps = []
+        for b in range(BLOCKS):
+            pool_ps.append(bank(f"pool_ps_{b}"))
+            for c in range(CHAINS):
+                flip(pool_ps[b][:, 0:BLOCK], sums[b, c][:], start=(c == 0), stop=(c == CHAINS - 1))
 
-        for h in range(HALVES):
-            hidden = [held.tile([P, BLOCK], BF16, name=f"hidden_{h}_{b}") for b in range(BLOCKS)]
-            elu(nc, held, [t[:] for t in hidden], [t[:, 0:BLOCK] for t in pool_ps[h]], f"hidden_{h}")
-            out_ps = [bank(f"out_ps_{h}_{b}") for b in range(BLOCKS)]
-            for b in range(BLOCKS):
-                nc.tensor.matmul(out_ps[b][:, 0:BLOCK], w2_sb[:], hidden[b][:], start=True, stop=True)
-            out_sb = [held.tile([P, BLOCK], F32, name=f"out_sb_{h}_{b}") for b in range(BLOCKS)]
-            elu(nc, held, [t[:] for t in out_sb], [t[:, 0:BLOCK] for t in out_ps], f"out_{h}")
-            for b in range(BLOCKS):
-                at = h * HALF + b * BLOCK
-                nc.sync.dma_start(out[:, at : at + BLOCK], out_sb[b][:])
+        hidden = [held.tile([P, BLOCK], BF16, name=f"hidden_{b}") for b in range(BLOCKS)]
+        elu(nc, held, [t[:] for t in hidden], [t[:, 0:BLOCK] for t in pool_ps], "hidden")
+        out_ps = [bank(f"out_ps_{b}") for b in range(BLOCKS)]
+        for b in range(BLOCKS):
+            nc.tensor.matmul(out_ps[b][:, 0:BLOCK], w2_sb[:], hidden[b][:], start=True, stop=True)
+        out_sb = [held.tile([P, BLOCK], F32, name=f"out_sb_{b}") for b in range(BLOCKS)]
+        elu(nc, held, [t[:] for t in out_sb], [t[:, 0:BLOCK] for t in out_ps], "out")
+        for b in range(BLOCKS):
+            nc.sync.dma_start(out[:, b * BLOCK : (b + 1) * BLOCK], out_sb[b][:])

@@ -15,8 +15,8 @@ BLOCKS = EDGES // BLOCK
 BANK = 512
 PSUM_BANKS = 8
 PER_BANK = BANK // P
-CHAINS = 3
-LINKS = MEMBERS // CHAINS
+SUMS_BY_VECTOR = ((0, 1), (2, 3), (4, 5))
+SUMS_BY_BOTH = ((0, 1), (2, 3), (4,), (5,))
 TABLE_LOADS = 4
 REPEAT = 64
 SLOPE = 0.2
@@ -95,26 +95,22 @@ def tile_hypergat_kernel(tc, table, w, att, w2, offs, out):
         def flip(result, block, start, stop, counted=False):
             nc.tensor.matmul(result, block, identity[:], is_transpose=not counted, start=start, stop=stop)
 
-        lead = [bank(f"lead_{n}") for n in range(BLOCKS * CHAINS // PER_BANK)]
-        rest = [bank(f"rest_{n}") for n in range(BLOCKS * (MEMBERS - CHAINS) // PER_BANK)]
-
-        def flipped(b, a):
-            c, i = divmod(a, LINKS)
-            if i == 0:
-                n, slot = divmod(b * CHAINS + c, PER_BANK)
-                return lead[n][:, slot * P : (slot + 1) * P]
-            n, slot = divmod((b * CHAINS + c) * (LINKS - 1) + i - 1, PER_BANK)
-            return rest[n][:, slot * P : (slot + 1) * P]
-
+        running = [SUMS_BY_VECTOR if b == 0 else SUMS_BY_BOTH for b in range(BLOCKS)]
+        firsts = [[run[0] for run in running[b]] for b in range(BLOCKS)]
+        seconds = [[run[1] for run in running[b] if len(run) > 1] for b in range(BLOCKS)]
+        by_scalar = [(b, a) for b in range(1, BLOCKS) for a in firsts[b]]
+        by_vector = [(0, a) for a in firsts[0]] + [(b, a) for b in range(BLOCKS) for a in seconds[b]]
+        flipped = {}
+        for reader, blocks in (("scalar", by_scalar), ("vector", by_vector)):
+            for k, block in enumerate(blocks):
+                if k % PER_BANK == 0:
+                    flips = bank(f"flips_{reader}_{k // PER_BANK}")
+                flipped[block] = flips[:, k % PER_BANK * P : (k % PER_BANK + 1) * P]
         for b in range(BLOCKS):
-            for a in range(MEMBERS):
-                flip(
-                    flipped(b, a),
-                    y_f32[a][:, b * BLOCK : (b + 1) * BLOCK],
-                    start=True,
-                    stop=True,
-                    counted=(a == MEMBERS - 1),
-                )
+            last = b == BLOCKS - 1
+            for a in seconds[b] + firsts[b] if last else firsts[b] + seconds[b]:
+                block = y_f32[a][:, b * BLOCK : (b + 1) * BLOCK]
+                flip(flipped[b, a], block, start=True, stop=True, counted=last and a in firsts[b])
 
         def by_block(tile):
             return tile[:].rearrange("p (b a) -> p b a", a=MEMBERS)
@@ -144,25 +140,29 @@ def tile_hypergat_kernel(tc, table, w, att, w2, offs, out):
             by_block(weight), by_block(grown), inverse[:].unsqueeze(2).to_broadcast([P, BLOCKS, MEMBERS])
         )
 
+        def column(b, a):
+            return weight[:, b * MEMBERS + a : b * MEMBERS + a + 1]
+
         sums = {}
-        for i in range(LINKS):
-            for b in range(BLOCKS):
-                for c in range(CHAINS):
-                    a = c * LINKS + i
-                    column = weight[:, b * MEMBERS + a : b * MEMBERS + a + 1]
-                    longer = held.tile([P, P], F32, name=f"sum_{b}_{c}_{i}")
-                    if i == 0:
-                        nc.scalar.activation(longer[:], flipped(b, a), ACT.Copy, scale=column)
-                    else:
-                        nc.vector.scalar_tensor_tensor(
-                            longer[:], flipped(b, a), column, sums[b, c][:], op0=ALU.mult, op1=ALU.add
-                        )
-                    sums[b, c] = longer
+        for b in range(BLOCKS):
+            for a in firsts[b]:
+                sums[b, a] = held.tile([P, P], F32, name=f"first_{b}_{a}")
+                if b == 0:
+                    nc.vector.tensor_scalar_mul(sums[b, a][:], flipped[b, a], column(b, a))
+                else:
+                    nc.scalar.activation(sums[b, a][:], flipped[b, a], ACT.Copy, scale=column(b, a))
+        for b in range(BLOCKS):
+            for first, second in [run for run in running[b] if len(run) > 1]:
+                both = held.tile([P, P], F32, name=f"both_{b}_{first}")
+                nc.vector.scalar_tensor_tensor(
+                    both[:], flipped[b, second], column(b, second), sums[b, first][:], op0=ALU.mult, op1=ALU.add
+                )
+                sums[b, first] = both
         pool_ps = []
         for b in range(BLOCKS):
             pool_ps.append(bank(f"pool_ps_{b}"))
-            for c in range(CHAINS):
-                flip(pool_ps[b][:, 0:BLOCK], sums[b, c][:], start=(c == 0), stop=(c == CHAINS - 1))
+            for a in firsts[b]:
+                flip(pool_ps[b][:, 0:BLOCK], sums[b, a][:], start=(a == firsts[b][0]), stop=(a == firsts[b][-1]))
 
         hidden = [held.tile([P, BLOCK], BF16, name=f"hidden_{b}") for b in range(BLOCKS)]
         elu(nc, held, [t[:] for t in hidden], [t[:, 0:BLOCK] for t in pool_ps], "hidden")

@@ -14,7 +14,6 @@ BLOCK = 128
 BLOCKS = EDGES // BLOCK
 BANK = 512
 PSUM_BANKS = 8
-PER_BANK = BANK // P
 SUMS_BY_VECTOR = ((0, 1), (2, 3), (4, 5))
 SUMS_BY_BOTH = ((0, 1), (2, 3), (4,), (5,))
 TABLE_LOADS = 4
@@ -102,15 +101,15 @@ def tile_hypergat_kernel(tc, table, w, att, w2, offs, out):
         by_vector = [(0, a) for a in firsts[0]] + [(b, a) for b in range(BLOCKS) for a in seconds[b]]
         flipped = {}
         for reader, blocks in (("scalar", by_scalar), ("vector", by_vector)):
-            for k, block in enumerate(blocks):
-                if k % PER_BANK == 0:
-                    flips = bank(f"flips_{reader}_{k // PER_BANK}")
-                flipped[block] = flips[:, k % PER_BANK * P : (k % PER_BANK + 1) * P]
-        for b in range(BLOCKS):
-            last = b == BLOCKS - 1
-            for a in seconds[b] + firsts[b] if last else firsts[b] + seconds[b]:
-                block = y_f32[a][:, b * BLOCK : (b + 1) * BLOCK]
-                flip(flipped[b, a], block, start=True, stop=True, counted=last and a in firsts[b])
+            for n, (start, stop) in enumerate(((0, 4), (4, 8), (8, 10), (10, 12))):
+                flips = bank(f"flips_{reader}_{n}")
+                for k, block in enumerate(blocks[start:stop]):
+                    flipped[block] = flips[:, k * P : (k + 1) * P]
+        last = by_scalar[-2:] + by_vector[-2:]
+        to_flip = [(b, a) for b in range(BLOCKS) for a in firsts[b] + seconds[b] if (b, a) not in last]
+        for b, a in to_flip + last:
+            block = y_f32[a][:, b * BLOCK : (b + 1) * BLOCK]
+            flip(flipped[b, a], block, start=True, stop=True, counted=(b, a) in last)
 
         def by_block(tile):
             return tile[:].rearrange("p (b a) -> p b a", a=MEMBERS)
@@ -161,8 +160,9 @@ def tile_hypergat_kernel(tc, table, w, att, w2, offs, out):
         pool_ps = []
         for b in range(BLOCKS):
             pool_ps.append(bank(f"pool_ps_{b}"))
-            for a in firsts[b]:
-                flip(pool_ps[b][:, 0:BLOCK], sums[b, a][:], start=(a == firsts[b][0]), stop=(a == firsts[b][-1]))
+            order = sorted(running[b], key=len)
+            for run in order:
+                flip(pool_ps[b][:, 0:BLOCK], sums[b, run[0]][:], start=(run == order[0]), stop=(run == order[-1]))
 
         hidden = [held.tile([P, BLOCK], BF16, name=f"hidden_{b}") for b in range(BLOCKS)]
         elu(nc, held, [t[:] for t in hidden], [t[:, 0:BLOCK] for t in pool_ps], "hidden")

@@ -14,8 +14,8 @@ BLOCK = 128
 BLOCKS = EDGES // BLOCK
 BANK = 512
 PSUM_BANKS = 8
-SUMS_BY_VECTOR = ((0, 1), (2, 3), (4, 5))
-SUMS_BY_BOTH = ((0, 1), (2, 3), (4,), (5,))
+PAIRS = ((0, 1), (2, 3), (4, 5))
+PER_BANK = BANK // P
 TABLE_LOADS = 4
 REPEAT = 64
 SLOPE = 0.2
@@ -94,20 +94,18 @@ def tile_hypergat_kernel(tc, table, w, att, w2, offs, out):
         def flip(result, block, start, stop, counted=False):
             nc.tensor.matmul(result, block, identity[:], is_transpose=not counted, start=start, stop=stop)
 
-        running = [SUMS_BY_VECTOR if b == 0 else SUMS_BY_BOTH for b in range(BLOCKS)]
-        firsts = [[run[0] for run in running[b]] for b in range(BLOCKS)]
-        seconds = [[run[1] for run in running[b] if len(run) > 1] for b in range(BLOCKS)]
-        by_scalar = [(b, a) for b in range(1, BLOCKS) for a in firsts[b]]
-        by_vector = [(0, a) for a in firsts[0]] + [(b, a) for b in range(BLOCKS) for a in seconds[b]]
+        by_scalar = [(b, first) for b in range(1, BLOCKS) for first, _ in PAIRS]
+        by_vector = [(0, first) for first, _ in PAIRS] + [(b, second) for b in range(BLOCKS) for _, second in PAIRS]
         flipped = {}
         for reader, blocks in (("scalar", by_scalar), ("vector", by_vector)):
-            for n, (start, stop) in enumerate(((0, 4), (4, 8), (8, 10), (10, 12))):
-                flips = bank(f"flips_{reader}_{n}")
+            starts = [*range(0, len(blocks) - 2, PER_BANK), len(blocks) - 2, len(blocks)]
+            for start, stop in zip(starts, starts[1:]):
+                flips = bank(f"flips_{reader}_{start}")
                 for k, block in enumerate(blocks[start:stop]):
                     flipped[block] = flips[:, k * P : (k + 1) * P]
         last = by_scalar[-2:] + by_vector[-2:]
-        to_flip = [(b, a) for b in range(BLOCKS) for a in firsts[b] + seconds[b] if (b, a) not in last]
-        for b, a in to_flip + last:
+        every = [(b, a) for b in range(BLOCKS) for a in [first for first, _ in PAIRS] + [second for _, second in PAIRS]]
+        for b, a in [block for block in every if block not in last] + last:
             block = y_f32[a][:, b * BLOCK : (b + 1) * BLOCK]
             flip(flipped[b, a], block, start=True, stop=True, counted=(b, a) in last)
 
@@ -139,30 +137,41 @@ def tile_hypergat_kernel(tc, table, w, att, w2, offs, out):
             by_block(weight), by_block(grown), inverse[:].unsqueeze(2).to_broadcast([P, BLOCKS, MEMBERS])
         )
 
-        def column(b, a):
-            return weight[:, b * MEMBERS + a : b * MEMBERS + a + 1]
+        def column(tile, b, a):
+            return tile[:, b * MEMBERS + a : b * MEMBERS + a + 1]
 
+        singles = {}
+        for b in range(BLOCKS):
+            for a, _ in PAIRS:
+                singles[b, a] = held.tile([P, P], F32, name=f"single_{b}_{a}")
+                if b == 0:
+                    nc.vector.tensor_scalar(
+                        singles[b, a][:],
+                        flipped[b, a],
+                        column(grown, b, a),
+                        inverse[:, b : b + 1],
+                        op0=ALU.mult,
+                        op1=ALU.mult,
+                    )
+                else:
+                    nc.scalar.activation(singles[b, a][:], flipped[b, a], ACT.Copy, scale=column(weight, b, a))
         sums = {}
         for b in range(BLOCKS):
-            for a in firsts[b]:
-                sums[b, a] = held.tile([P, P], F32, name=f"first_{b}_{a}")
-                if b == 0:
-                    nc.vector.tensor_scalar_mul(sums[b, a][:], flipped[b, a], column(b, a))
-                else:
-                    nc.scalar.activation(sums[b, a][:], flipped[b, a], ACT.Copy, scale=column(b, a))
-        for b in range(BLOCKS):
-            for first, second in [run for run in running[b] if len(run) > 1]:
-                both = held.tile([P, P], F32, name=f"both_{b}_{first}")
+            for first, a in PAIRS:
+                sums[b, first] = held.tile([P, P], F32, name=f"sum_{b}_{first}")
                 nc.vector.scalar_tensor_tensor(
-                    both[:], flipped[b, second], column(b, second), sums[b, first][:], op0=ALU.mult, op1=ALU.add
+                    sums[b, first][:],
+                    flipped[b, a],
+                    column(weight, b, a),
+                    singles[b, first][:],
+                    op0=ALU.mult,
+                    op1=ALU.add,
                 )
-                sums[b, first] = both
         pool_ps = []
         for b in range(BLOCKS):
             pool_ps.append(bank(f"pool_ps_{b}"))
-            order = sorted(running[b], key=len)
-            for run in order:
-                flip(pool_ps[b][:, 0:BLOCK], sums[b, run[0]][:], start=(run == order[0]), stop=(run == order[-1]))
+            for k, (first, _) in enumerate(PAIRS):
+                flip(pool_ps[b][:, 0:BLOCK], sums[b, first][:], start=(k == 0), stop=(k == len(PAIRS) - 1))
 
         hidden = [held.tile([P, BLOCK], BF16, name=f"hidden_{b}") for b in range(BLOCKS)]
         elu(nc, held, [t[:] for t in hidden], [t[:, 0:BLOCK] for t in pool_ps], "hidden")

@@ -23,15 +23,15 @@ SLOPE = 0.2
 FLOPS = 2 * P * P * MEMBERS * EDGES + 2 * P * MEMBERS * EDGES + 2 * P * P * EDGES
 
 
-def elu(nc, pool, results, values, name):
-    grown, kept = [], []
+def elu_terms(nc, pool, values, kept_dtype, name):
+    terms = []
     for i, value in enumerate(values):
-        grown.append(pool.tile([P, BLOCK], F32, name=f"{name}_grown_{i}"))
-        nc.scalar.activation(grown[i][:], value, ACT.Exp)
-        kept.append(pool.tile([P, BLOCK], F32, name=f"{name}_kept_{i}"))
-        nc.scalar.activation(kept[i][:], value, ACT.Relu)
-    for i, result in enumerate(results):
-        nc.vector.scalar_tensor_tensor(result, grown[i][:], -1.0, kept[i][:], op0=ALU.add, op1=ALU.min)
+        grown = pool.tile([P, BLOCK], F32, name=f"{name}_grown_{i}")
+        nc.scalar.activation(grown[:], value, ACT.Exp)
+        kept = pool.tile([P, BLOCK], kept_dtype, name=f"{name}_kept_{i}")
+        nc.scalar.activation(kept[:], value, ACT.Relu)
+        terms.append((grown, kept))
+    return terms
 
 
 def tile_hypergat_kernel(tc, table, w, att, w2, offs, out):
@@ -173,12 +173,16 @@ def tile_hypergat_kernel(tc, table, w, att, w2, offs, out):
             for k, (first, _) in enumerate(PAIRS):
                 flip(pool_ps[b][:, 0:BLOCK], sums[b, first][:], start=(k == 0), stop=(k == len(PAIRS) - 1))
 
-        hidden = [held.tile([P, BLOCK], BF16, name=f"hidden_{b}") for b in range(BLOCKS)]
-        elu(nc, held, [t[:] for t in hidden], [t[:, 0:BLOCK] for t in pool_ps], "hidden")
-        out_ps = [bank(f"out_ps_{b}") for b in range(BLOCKS)]
-        for b in range(BLOCKS):
-            nc.tensor.matmul(out_ps[b][:, 0:BLOCK], w2_sb[:], hidden[b][:], start=True, stop=True)
-        out_sb = [held.tile([P, BLOCK], F32, name=f"out_sb_{b}") for b in range(BLOCKS)]
-        elu(nc, held, [t[:] for t in out_sb], [t[:, 0:BLOCK] for t in out_ps], "out")
-        for b in range(BLOCKS):
-            nc.sync.dma_start(out[:, b * BLOCK : (b + 1) * BLOCK], out_sb[b][:])
+        terms = elu_terms(nc, held, [t[:, 0:BLOCK] for t in pool_ps], BF16, "hidden")
+        out_ps = []
+        for b, (grown_b, kept) in enumerate(terms):
+            under = held.tile([P, BLOCK], BF16, name=f"hidden_under_{b}")
+            nc.vector.tensor_scalar(under[:], grown_b[:], -1.0, 0.0, op0=ALU.add, op1=ALU.min)
+            out_ps.append(bank(f"out_ps_{b}"))
+            nc.tensor.matmul(out_ps[b][:, 0:BLOCK], w2_sb[:], kept[:], start=True, stop=False)
+            nc.tensor.matmul(out_ps[b][:, 0:BLOCK], w2_sb[:], under[:], start=False, stop=True)
+        terms = elu_terms(nc, held, [t[:, 0:BLOCK] for t in out_ps], F32, "out")
+        for b, (grown_b, kept) in enumerate(terms):
+            out_sb = held.tile([P, BLOCK], F32, name=f"out_sb_{b}")
+            nc.vector.scalar_tensor_tensor(out_sb[:], grown_b[:], -1.0, kept[:], op0=ALU.add, op1=ALU.min)
+            nc.sync.dma_start(out[:, b * BLOCK : (b + 1) * BLOCK], out_sb[:])

@@ -14,7 +14,7 @@ BLOCK = 128
 BLOCKS = EDGES // BLOCK
 BANK = 512
 PSUM_BANKS = 8
-PAIRS = ((0, 1), (2, 3), (4, 5))
+SUMS = [((0, 1), (2, 3), (4, 5))] * (BLOCKS - 1) + [((0, 1), (2, 3), (4,), (5,))]
 PER_BANK = BANK // P
 TABLE_LOADS = 4
 REPEAT = 64
@@ -94,8 +94,10 @@ def tile_hypergat_kernel(tc, table, w, att, w2, offs, out):
         def flip(result, block, start, stop, counted=False):
             nc.tensor.matmul(result, block, identity[:], is_transpose=not counted, start=start, stop=stop)
 
-        by_scalar = [(b, first) for b in range(1, BLOCKS) for first, _ in PAIRS]
-        by_vector = [(0, first) for first, _ in PAIRS] + [(b, second) for b in range(BLOCKS) for _, second in PAIRS]
+        firsts = [[run[0] for run in SUMS[b]] for b in range(BLOCKS)]
+        seconds = [[run[1] for run in SUMS[b] if len(run) > 1] for b in range(BLOCKS)]
+        by_scalar = [(b, a) for b in range(1, BLOCKS) for a in firsts[b]]
+        by_vector = [(0, a) for a in firsts[0]] + [(b, a) for b in range(BLOCKS) for a in seconds[b]]
         flipped = {}
         for reader, blocks in (("scalar", by_scalar), ("vector", by_vector)):
             starts = [*range(0, len(blocks) - 2, PER_BANK), len(blocks) - 2, len(blocks)]
@@ -104,8 +106,11 @@ def tile_hypergat_kernel(tc, table, w, att, w2, offs, out):
                 for k, block in enumerate(blocks[start:stop]):
                     flipped[block] = flips[:, k * P : (k + 1) * P]
         last = by_scalar[-2:] + by_vector[-2:]
-        every = [(b, a) for b in range(BLOCKS) for a in [first for first, _ in PAIRS] + [second for _, second in PAIRS]]
-        for b, a in [block for block in every if block not in last] + last:
+        turns = []
+        for b in range(BLOCKS + 1):
+            turns += [(b, a) for a in firsts[b]] if b < BLOCKS else []
+            turns += [(b - 1, a) for a in seconds[b - 1]] if b > 0 else []
+        for b, a in [block for block in turns if block not in last] + last:
             block = y_f32[a][:, b * BLOCK : (b + 1) * BLOCK]
             flip(flipped[b, a], block, start=True, stop=True, counted=(b, a) in last)
 
@@ -140,13 +145,13 @@ def tile_hypergat_kernel(tc, table, w, att, w2, offs, out):
         def column(tile, b, a):
             return tile[:, b * MEMBERS + a : b * MEMBERS + a + 1]
 
-        singles = {}
+        sums = {}
         for b in range(BLOCKS):
-            for a, _ in PAIRS:
-                singles[b, a] = held.tile([P, P], F32, name=f"single_{b}_{a}")
+            for a in firsts[b]:
+                sums[b, a] = held.tile([P, P], F32, name=f"first_{b}_{a}")
                 if b == 0:
                     nc.vector.tensor_scalar(
-                        singles[b, a][:],
+                        sums[b, a][:],
                         flipped[b, a],
                         column(grown, b, a),
                         inverse[:, b : b + 1],
@@ -154,24 +159,25 @@ def tile_hypergat_kernel(tc, table, w, att, w2, offs, out):
                         op1=ALU.mult,
                     )
                 else:
-                    nc.scalar.activation(singles[b, a][:], flipped[b, a], ACT.Copy, scale=column(weight, b, a))
-        sums = {}
+                    nc.scalar.activation(sums[b, a][:], flipped[b, a], ACT.Copy, scale=column(weight, b, a))
         for b in range(BLOCKS):
-            for first, a in PAIRS:
-                sums[b, first] = held.tile([P, P], F32, name=f"sum_{b}_{first}")
+            for first, second in [run for run in SUMS[b] if len(run) > 1]:
+                both = held.tile([P, P], F32, name=f"both_{b}_{first}")
                 nc.vector.scalar_tensor_tensor(
+                    both[:],
+                    flipped[b, second],
+                    column(weight, b, second),
                     sums[b, first][:],
-                    flipped[b, a],
-                    column(weight, b, a),
-                    singles[b, first][:],
                     op0=ALU.mult,
                     op1=ALU.add,
                 )
+                sums[b, first] = both
         pool_ps = []
         for b in range(BLOCKS):
             pool_ps.append(bank(f"pool_ps_{b}"))
-            for k, (first, _) in enumerate(PAIRS):
-                flip(pool_ps[b][:, 0:BLOCK], sums[b, first][:], start=(k == 0), stop=(k == len(PAIRS) - 1))
+            order = sorted(SUMS[b], key=len)
+            for run in order:
+                flip(pool_ps[b][:, 0:BLOCK], sums[b, run[0]][:], start=(run == order[0]), stop=(run == order[-1]))
 
         terms = elu_terms(nc, held, [t[:, 0:BLOCK] for t in pool_ps], BF16, "hidden")
         out_ps = []

import concourse.mybir as mybir
from concourse.masks import make_identity

BF16, F32, U16 = mybir.dt.bfloat16, mybir.dt.float32, mybir.dt.uint16
ACT = mybir.ActivationFunctionType
ALU = mybir.AluOpType
AXIS = mybir.AxisListType

P = 128
NODES = 4096
EDGES = 512
MEMBERS = 6
BLOCK = 128
BLOCKS = EDGES // BLOCK
BANK = 512
PSUM_BANKS = 8
SUMS = [((0, 1), (2, 3), (4, 5))] * (BLOCKS - 1) + [((0, 1), (2, 3), (4,), (5,))]
PER_BANK = BANK // P
TABLE_LOADS = 4
REPEAT = 64
SLOPE = 0.2

FLOPS = 2 * P * P * MEMBERS * EDGES + 2 * P * MEMBERS * EDGES + 2 * P * P * EDGES


def elu_terms(nc, pool, values, kept_dtype, name):
    terms = []
    for i, value in enumerate(values):
        grown = pool.tile([P, BLOCK], F32, name=f"{name}_grown_{i}")
        nc.scalar.activation(grown[:], value, ACT.Exp)
        kept = pool.tile([P, BLOCK], kept_dtype, name=f"{name}_kept_{i}")
        nc.scalar.activation(kept[:], value, ACT.Relu)
        terms.append((grown, kept))
    return terms


def tile_hypergat_kernel(tc, table, w, att, w2, offs, out):
    nc = tc.nc
    with (
        tc.tile_pool(name="held", bufs=1) as held,
        tc.psum_pool(name="psum", bufs=1) as psum,
    ):

        def bank(name):
            return psum.tile([P, BANK], F32, name=name, tag="bank", bufs=PSUM_BANKS)

        offsets = held.tile([P, MEMBERS * EDGES // 16], U16, name="offsets")
        nc.sync.dma_start(offsets[:], offs)
        w_sb = held.tile([P, P], BF16, name="w_sb")
        nc.scalar.dma_start(w_sb[:], w)
        table_sb = held.tile([P, NODES], BF16, name="table_sb")
        part = NODES // TABLE_LOADS
        for i in range(TABLE_LOADS):
            queue = nc.sync if i % 2 == 0 else nc.scalar
            queue.dma_start(table_sb[:, i * part : (i + 1) * part], table[:, i * part : (i + 1) * part])
        att_sb = held.tile([P, 1], BF16, name="att_sb")
        nc.sync.dma_start(att_sb[:], att)
        w2_sb = held.tile([P, P], BF16, name="w2_sb")
        nc.scalar.dma_start(w2_sb[:], w2)
        identity = held.tile([P, P], F32, name="identity")
        make_identity(nc, identity[:])

        zero = held.tile([P, 1], F32, name="zero")
        nc.vector.memset(zero[:], 0.0)
        one = held.tile([P, 1], F32, name="one")
        nc.scalar.activation(one[:], zero[:], ACT.Exp)
        att_wide = held.tile([P, REPEAT], BF16, name="att_wide")
        nc.vector.tensor_copy(att_wide[:], att_sb[:].to_broadcast([P, REPEAT]))

        y_f32 = []
        y_bf16 = []
        for a in range(MEMBERS):
            picked = table_sb[:].indirect(offsets[:, a * EDGES // 16 : (a + 1) * EDGES // 16])
            y_ps = bank(f"y_ps_{a}")
            nc.tensor.matmul(y_ps[:], w_sb[:], picked, start=True, stop=True)
            y_bf16.append(held.tile([P, EDGES], BF16, name=f"y_bf16_{a}"))
            nc.vector.tensor_copy(y_bf16[a][:], y_ps[:])
            y_f32.append(held.tile([P, EDGES], F32, name=f"y_f32_{a}"))
            nc.scalar.copy(y_f32[a][:], y_ps[:])

        scores_ps = bank("scores_ps")
        for a in range(MEMBERS):
            for b in range(BLOCKS):
                col = a * BLOCKS + b
                nc.tensor.matmul(
                    scores_ps[:, col : col + REPEAT],
                    y_bf16[a][:, b * BLOCK : (b + 1) * BLOCK],
                    att_wide[:],
                    start=True,
                    stop=True,
                )
        scores = scores_ps[:, 0 : MEMBERS * BLOCKS].rearrange("p (a b) -> p b a", b=BLOCKS)

        def flip(result, block, start, stop, counted=False):
            nc.tensor.matmul(result, block, identity[:], is_transpose=not counted, start=start, stop=stop)

        firsts = [[run[0] for run in SUMS[b]] for b in range(BLOCKS)]
        seconds = [[run[1] for run in SUMS[b] if len(run) > 1] for b in range(BLOCKS)]
        by_scalar = [(b, a) for b in range(1, BLOCKS) for a in firsts[b]]
        by_vector = [(0, a) for a in firsts[0]] + [(b, a) for b in range(BLOCKS) for a in seconds[b]]
        flipped = {}
        for reader, blocks in (("scalar", by_scalar), ("vector", by_vector)):
            starts = [*range(0, len(blocks) - 2, PER_BANK), len(blocks) - 2, len(blocks)]
            for start, stop in zip(starts, starts[1:]):
                flips = bank(f"flips_{reader}_{start}")
                for k, block in enumerate(blocks[start:stop]):
                    flipped[block] = flips[:, k * P : (k + 1) * P]
        last = by_scalar[-2:] + by_vector[-2:]
        turns = []
        for b in range(BLOCKS + 1):
            turns += [(b, a) for a in firsts[b]] if b < BLOCKS else []
            turns += [(b - 1, a) for a in seconds[b - 1]] if b > 0 else []
        for b, a in [block for block in turns if block not in last] + last:
            block = y_f32[a][:, b * BLOCK : (b + 1) * BLOCK]
            flip(flipped[b, a], block, start=True, stop=True, counted=(b, a) in last)

        def by_block(tile):
            return tile[:].rearrange("p (b a) -> p b a", a=MEMBERS)

        neg_top = held.tile([P, BLOCKS], F32, name="neg_top")
        nc.vector.reduce_max(neg_top[:], scores, axis=AXIS.X, negate=True)
        damped = held.tile([P, BLOCKS * MEMBERS], F32, name="damped")
        nc.vector.tensor_scalar_mul(by_block(damped), scores, SLOPE)
        neg_peak = held.tile([P, BLOCKS], F32, name="neg_peak")
        nc.vector.scalar_tensor_tensor(neg_peak[:], neg_top[:], SLOPE, neg_top[:], op0=ALU.mult, op1=ALU.min)
        leaky = held.tile([P, BLOCKS * MEMBERS], F32, name="leaky")
        nc.vector.tensor_max(by_block(leaky), scores, by_block(damped))
        grown = held.tile([P, BLOCKS * MEMBERS], F32, name="grown")
        total = held.tile([P, BLOCKS], F32, name="total")
        for b in range(BLOCKS):
            nc.scalar.activation(
                grown[:, b * MEMBERS : (b + 1) * MEMBERS],
                leaky[:, b * MEMBERS : (b + 1) * MEMBERS],
                ACT.Exp,
                bias=neg_peak[:, b : b + 1],
                accum_out=total[:, b : b + 1],
            )
        inverse = held.tile([P, BLOCKS], F32, name="inverse")
        nc.vector.reciprocal(inverse[:], total[:])
        weight = held.tile([P, BLOCKS * MEMBERS], F32, name="weight")
        nc.vector.tensor_mul(
            by_block(weight), by_block(grown), inverse[:].unsqueeze(2).to_broadcast([P, BLOCKS, MEMBERS])
        )

        def column(tile, b, a):
            return tile[:, b * MEMBERS + a : b * MEMBERS + a + 1]

        sums = {}
        for b in range(BLOCKS):
            for a in firsts[b]:
                sums[b, a] = held.tile([P, P], F32, name=f"first_{b}_{a}")
                if b == 0:
                    nc.vector.tensor_scalar(
                        sums[b, a][:],
                        flipped[b, a],
                        column(grown, b, a),
                        inverse[:, b : b + 1],
                        op0=ALU.mult,
                        op1=ALU.mult,
                    )
                else:
                    nc.scalar.activation(sums[b, a][:], flipped[b, a], ACT.Copy, scale=column(weight, b, a))
        for b in range(BLOCKS):
            for first, second in [run for run in SUMS[b] if len(run) > 1]:
                both = held.tile([P, P], F32, name=f"both_{b}_{first}")
                nc.vector.scalar_tensor_tensor(
                    both[:],
                    flipped[b, second],
                    column(weight, b, second),
                    sums[b, first][:],
                    op0=ALU.mult,
                    op1=ALU.add,
                )
                sums[b, first] = both
        pool_ps = []
        for b in range(BLOCKS):
            pool_ps.append(bank(f"pool_ps_{b}"))
            order = sorted(SUMS[b], key=len)
            for run in order:
                flip(pool_ps[b][:, 0:BLOCK], sums[b, run[0]][:], start=(run == order[0]), stop=(run == order[-1]))

        terms = elu_terms(nc, held, [t[:, 0:BLOCK] for t in pool_ps], BF16, "hidden")
        out_ps = []
        for b, (grown_b, kept) in enumerate(terms):
            under = held.tile([P, BLOCK], BF16, name=f"hidden_under_{b}")
            nc.vector.tensor_scalar(under[:], grown_b[:], -1.0, 0.0, op0=ALU.add, op1=ALU.min)
            out_ps.append(bank(f"out_ps_{b}"))
            nc.tensor.matmul(out_ps[b][:, 0:BLOCK], w2_sb[:], kept[:], start=True, stop=False)
            nc.tensor.matmul(out_ps[b][:, 0:BLOCK], w2_sb[:], under[:], start=False, stop=True)
        terms = elu_terms(nc, held, [t[:, 0:BLOCK] for t in out_ps], F32, "out")
        for b, (grown_b, kept) in enumerate(terms):
            out_sb = held.tile([P, BLOCK], F32, name=f"out_sb_{b}")
            nc.vector.scalar_tensor_tensor(out_sb[:], grown_b[:], -1.0, kept[:], op0=ALU.add, op1=ALU.min)
            nc.sync.dma_start(out[:, b * BLOCK : (b + 1) * BLOCK], out_sb[:])
